import numpy as np
import ml_dtypes


def mxq(x, axis, fmt="e4m3"):
    dtype, down = {"e4m3": (ml_dtypes.float8_e4m3fn, 7), "e5m2": (ml_dtypes.float8_e5m2, 14)}[fmt]
    v = np.moveaxis(np.asarray(x, np.float32).astype(ml_dtypes.bfloat16).astype(np.float64), axis, -1)
    blocks = v.reshape(v.shape[:-1] + (-1, 32))
    amax = np.abs(blocks).max(-1, keepdims=True)
    byte = np.maximum(np.where(amax > 0, np.frexp(amax)[1] - 1 + 127, 0) - down, 1)
    scale = np.exp2(byte - 127.0)
    codes = (blocks / scale).astype(np.float32).astype(dtype).astype(np.float64)
    return np.moveaxis((codes * scale).reshape(v.shape), -1, axis)


WIDE = False


def mx_kscale(k):
    if not WIDE:
        return np.ones(k)
    levels = np.array([10, -10, 5, -5, 0])
    a = np.random.permutation(np.resize(levels, k // 512 * 4)).reshape(k // 512, 4)
    idx = np.arange(k)
    return np.exp2(a[idx // 512, idx % 128 // 32])


BF16 = ml_dtypes.bfloat16


def bf(x):
    return np.asarray(x, np.float32).astype(BF16)


def f64(x):
    return np.asarray(x).astype(np.float64)


N, D, C, M = 3072, 512, 16, 16


def setup_inputs():
    s = mx_kscale(D)
    return {"x": bf(np.random.standard_normal((N, D)) * s),
            "x_var": bf(0.1 + 4.0 * np.random.standard_normal((N, D)) ** 2),
            "prototypes": bf(np.random.standard_normal((C, M, D)) * 0.5 / np.sqrt(D) / s),
            "proto_var": bf(0.1 + 4.0 * np.random.standard_normal((C, M, D)) ** 2)}


def reference(x, x_var, prototypes, proto_var):
    x, x_var, prototypes, proto_var = f64(x), f64(x_var), f64(prototypes), f64(proto_var)
    lamda = 1.0 / x.shape[-1]
    dot = (mxq(x, 1, "e4m3") @ mxq(prototypes.reshape(C * M, D), 1, "e4m3").T).reshape(N, C, M)
    cross = (mxq(np.sqrt(x_var), 1, "e4m3") @ mxq(np.sqrt(proto_var).reshape(C * M, D), 1, "e4m3").T).reshape(N, C, M)
    w2 = (2.0 - 2.0 * dot
          + lamda * (np.sum(x_var, axis=-1)[:, None, None]
                     + np.sum(proto_var, axis=-1)[None, :, :]
                     - 2.0 * cross))
    return -w2

@@ -1,0 +1,181 @@
+from contextlib import ExitStack
+
+import concourse.mybir as mybir
+from concourse.masks import make_identity
+
+F32 = mybir.dt.float32
+BF16 = mybir.dt.bfloat16
+U32 = mybir.dt.uint32
+U8 = mybir.dt.uint8
+FP8X4 = mybir.dt.float8_e4m3fn_x4
+ALU = mybir.AluOpType
+ACT = mybir.ActivationFunctionType
+
+P = 128
+N_PIX = 3072
+D = 512
+J = 256
+NT = N_PIX // P
+NU = NT // 2
+CHUNKS = (2, 2, 4, 4, 4, 4, 4)
+FLOPS = 2 * 2 * N_PIX * J * D
+
+
+def tile_probprotoseghead_kernel(tc, x, x_var, prototypes, proto_var, out):
+    nc = tc.nc
+    x_v = x.rearrange("(p t) d -> p t d", t=NT)
+    xv_v = x_var.rearrange("(p t) d -> p t d", t=NT)
+    out_v = out.rearrange("(p t) c m -> p t (c m)", t=NT)
+    p_v = prototypes.rearrange("(r c) m d -> (c m) r d", r=2)
+    pv_v = proto_var.rearrange("(r c) m d -> (c m) r d", r=2)
+
+    with ExitStack() as ctx:
+        keep = ctx.enter_context(tc.tile_pool(name="keep", bufs=1))
+        work = ctx.enter_context(tc.tile_pool(name="work", bufs=3))
+        psum = ctx.enter_context(tc.psum_pool(name="psum", bufs=2))
+
+        pv_sb = keep.tile([P, 2, D], BF16, name="pv_sb")
+        p_sb = keep.tile([P, 2, D], BF16, name="p_sb")
+        nc.sync.dma_start(out=pv_sb[:], in_=pv_v)
+        nc.sync.dma_start(out=p_sb[:], in_=p_v)
+        x_of = []
+        xv_of = []
+        t0 = 0
+        for c, size in enumerate(CHUNKS):
+            xv_c = keep.tile([P, size, D], BF16, name="xv%d" % c)
+            x_c = keep.tile([P, size, D], BF16, name="x%d" % c)
+            nc.sync.dma_start(out=xv_c[:], in_=xv_v[:, t0 : t0 + size, :])
+            nc.sync.dma_start(out=x_c[:], in_=x_v[:, t0 : t0 + size, :])
+            for k in range(size):
+                x_of.append(x_c[:, k, :])
+                xv_of.append(xv_c[:, k, :])
+            t0 += size
+
+        ident = keep.tile([P, P], F32, name="ident")
+        make_identity(nc, ident[:])
+
+        bn = keep.tile([P, NT], F32, name="bn")
+        spn = keep.tile([P, 2], F32, name="spn")
+        rep = keep.tile([P, 2, P], F32, name="rep")
+        bj = keep.tile([P, J], F32, name="bj")
+        gp = keep.tile([P, 2048], BF16, name="gp", align_bytes=64)
+        sq_tmp = keep.tile([P, 1024], BF16, name="sq_tmp")
+        p_codes = keep.tile([P, 512], U32, name="p_codes", align_bytes=64)
+        p_scl = keep.tile([P, 512], U8, name="p_scl", align_bytes=64)
+
+        def transposes(bank, rows):
+            for i in range(2):
+                words = rows[i].bitcast(F32)
+                for u in range(2):
+                    nc.tensor.transpose(bank[:, u, i, :], words[:, u * P : (u + 1) * P], ident[:])
+
+        def as_words(bank):
+            return bank[:].rearrange("p u i n -> p (i n) u")
+
+        def as_halves(bank):
+            return bank[:].bitcast(BF16).rearrange("p u i (n e) -> p (i n) u e", e=2)
+
+        def halves_out(ap):
+            return ap.rearrange("p (m u e) -> p m u e", u=2, e=2)
+
+        def row_sum(dst, rows):
+            junk = work.tile([P, D], BF16, tag="junk")
+            nc.vector.tensor_scalar(
+                out=junk[:], in0=rows, scalar1=-1.0 / D, scalar2=None,
+                op0=ALU.mult, op1=ALU.add, accum_out=dst,
+            )
+
+        pt = psum.tile([P, 2, 2, P], F32, tag="xt")
+        pvt = psum.tile([P, 2, 2, P], F32, tag="vt")
+        transposes(pvt, [pv_sb[:, 0, :], pv_sb[:, 1, :]])
+        transposes(pt, [p_sb[:, 0, :], p_sb[:, 1, :]])
+        nc.scalar.activation(out=halves_out(sq_tmp[:]), in_=as_halves(pvt), func=ACT.Sqrt)
+        for r in range(2):
+            row_sum(spn[:, r : r + 1], pv_sb[:, r, :])
+        for r in range(2):
+            nc.vector.tensor_copy(out=rep[:, r, :], in_=spn[:, r : r + 1].to_broadcast([P, P]))
+        nc.vector.tensor_scalar(
+            out=halves_out(gp[:, 0:1024]), in0=as_halves(pt), scalar1=2.0, scalar2=None, op0=ALU.mult
+        )
+        nc.vector.tensor_scalar(
+            out=gp[:, 1024:2048], in0=sq_tmp[:], scalar1=2.0 ** -8, scalar2=None, op0=ALU.mult
+        )
+        nc.vector.quantize_mx(out=p_codes[:].bitcast(FP8X4), scales=p_scl[:], in_=gp[:])
+
+        banks = {}
+        quant = {}
+        accs = {}
+
+        def stage_t(u):
+            xt = psum.tile([P, 2, 2, P], F32, tag="xt")
+            vt = psum.tile([P, 2, 2, P], F32, tag="vt")
+            transposes(vt, [xv_of[2 * u], xv_of[2 * u + 1]])
+            transposes(xt, [x_of[2 * u], x_of[2 * u + 1]])
+            banks[u] = (xt, vt)
+
+        def stage_s(u):
+            xt, vt = banks[u]
+            g = work.tile([P, 2048], BF16, tag="g", align_bytes=64)
+            nc.scalar.activation(out=halves_out(g[:, 1024:2048]), in_=as_halves(vt), func=ACT.Sqrt)
+            nc.scalar.copy(
+                out=g[:, 0:1024].bitcast(F32).rearrange("p (m u) -> p m u", u=2), in_=as_words(xt)
+            )
+            quant[u] = g
+
+        def stage_q(u):
+            g = quant[u]
+            codes = work.tile([P, 512], U32, tag="codes", align_bytes=64)
+            scl = work.tile([P, 512], U8, tag="scl", align_bytes=64)
+            nc.vector.quantize_mx(out=codes[:].bitcast(FP8X4), scales=scl[:], in_=g[:])
+            acc = psum.tile([P, 2, J], F32, tag="acc", bufs=3)
+            for i in range(2):
+                for h in range(2):
+                    cols = slice(256 * h + P * i, 256 * h + P * i + P)
+                    pcols = slice(256 * h, 256 * h + 256)
+                    nc.tensor.matmul_mx(
+                        out=acc[:, i, :],
+                        lhsT=codes[:, cols].bitcast(FP8X4),
+                        lhsT_scale=scl[:, cols],
+                        rhs=p_codes[:, pcols].bitcast(FP8X4),
+                        rhs_scale=p_scl[:, pcols],
+                        start=(h == 0),
+                        stop=(h == 1),
+                    )
+            accs[u] = acc
+
+        def stage_sum(u):
+            for i in range(2):
+                t = 2 * u + i
+                row_sum(bn[:, t : t + 1], xv_of[t])
+
+        def stage_e(u):
+            acc = accs[u]
+            o_sb = work.tile([P, 2, J], F32, tag="o", bufs=4)
+            for i in range(2):
+                t = 2 * u + i
+                nc.vector.scalar_tensor_tensor(
+                    out=o_sb[:, i, :], in0=acc[:, i, :], scalar=bn[:, t : t + 1], in1=bj[:],
+                    op0=ALU.add, op1=ALU.add,
+                )
+            nc.sync.dma_start(out=out_v[:, 2 * u : 2 * u + 2, :], in_=o_sb[:])
+
+        stage_t(0)
+        stage_sum(0)
+        bt = psum.tile([P, 2, P], F32, tag="bt", bufs=1)
+        for r in range(2):
+            nc.tensor.transpose(bt[:, r, :], rep[:, r, :], ident[:])
+        nc.vector.tensor_scalar(
+            out=bj[:], in0=bt[:].rearrange("p r n -> p (r n)"), scalar1=-2.0, scalar2=None, op0=ALU.add
+        )
+
+        for k in range(NU + 2):
+            if k + 1 < NU:
+                stage_t(k + 1)
+            if k < NU:
+                stage_s(k)
+            if 1 <= k <= NU:
+                stage_q(k - 1)
+            if k + 1 < NU:
+                stage_sum(k + 1)
+            if k >= 2:
+                stage_e(k - 2)

@@ -18,6 +18,8 @@ J = 256
 NT = N_PIX // P
 NU = NT // 2
 CHUNKS = (2, 2, 4, 4, 4, 4, 4)
+S_SUM_TILES = (7, 11, 15, 19)
+V_COPY_UNITS = ()
 FLOPS = 2 * 2 * N_PIX * J * D
 
 
@@ -33,6 +35,7 @@ def tile_probprotoseghead_kernel(tc, x, x_var, prototypes, proto_var, out):
         keep = ctx.enter_context(tc.tile_pool(name="keep", bufs=1))
         work = ctx.enter_context(tc.tile_pool(name="work", bufs=3))
         psum = ctx.enter_context(tc.psum_pool(name="psum", bufs=2))
+        ctx.enter_context(tc.manual_schedule())
 
         pv_sb = keep.tile([P, 2, D], BF16, name="pv_sb")
         p_sb = keep.tile([P, 2, D], BF16, name="p_sb")
@@ -54,7 +57,8 @@ def tile_probprotoseghead_kernel(tc, x, x_var, prototypes, proto_var, out):
         ident = keep.tile([P, P], F32, name="ident")
         make_identity(nc, ident[:])
 
-        bn = keep.tile([P, NT], F32, name="bn")
+        bn_v = keep.tile([P, NT], F32, name="bn_v")
+        bn_s = keep.tile([P, NT], F32, name="bn_s")
         spn = keep.tile([P, 2], F32, name="spn")
         rep = keep.tile([P, 2, P], F32, name="rep")
         bj = keep.tile([P, J], F32, name="bj")
@@ -78,37 +82,27 @@ def tile_probprotoseghead_kernel(tc, x, x_var, prototypes, proto_var, out):
         def halves_out(ap):
             return ap.rearrange("p (m u e) -> p m u e", u=2, e=2)
 
-        def row_sum(dst, rows):
-            junk = work.tile([P, D], BF16, tag="junk")
+        def words_out(ap):
+            return ap.bitcast(F32).rearrange("p (m u) -> p m u", u=2)
+
+        def row_sum_v(dst, rows):
+            junk = work.tile([P, D], BF16, tag="junk_v")
             nc.vector.tensor_scalar(
                 out=junk[:], in0=rows, scalar1=-1.0 / D, scalar2=None,
                 op0=ALU.mult, op1=ALU.add, accum_out=dst,
             )
 
-        pt = psum.tile([P, 2, 2, P], F32, tag="xt")
-        pvt = psum.tile([P, 2, 2, P], F32, tag="vt")
-        transposes(pvt, [pv_sb[:, 0, :], pv_sb[:, 1, :]])
-        transposes(pt, [p_sb[:, 0, :], p_sb[:, 1, :]])
-        nc.scalar.activation(out=halves_out(sq_tmp[:]), in_=as_halves(pvt), func=ACT.Sqrt)
-        for r in range(2):
-            row_sum(spn[:, r : r + 1], pv_sb[:, r, :])
-        for r in range(2):
-            nc.vector.tensor_copy(out=rep[:, r, :], in_=spn[:, r : r + 1].to_broadcast([P, P]))
-        nc.vector.tensor_scalar(
-            out=halves_out(gp[:, 0:1024]), in0=as_halves(pt), scalar1=2.0, scalar2=None, op0=ALU.mult
-        )
-        nc.vector.tensor_scalar(
-            out=gp[:, 1024:2048], in0=sq_tmp[:], scalar1=2.0 ** -8, scalar2=None, op0=ALU.mult
-        )
-        nc.vector.quantize_mx(out=p_codes[:].bitcast(FP8X4), scales=p_scl[:], in_=gp[:])
+        def row_sum_s(dst, rows):
+            junk = work.tile([P, D], BF16, tag="junk_s")
+            nc.scalar.activation(out=junk[:], in_=rows, func=ACT.Copy, scale=-1.0 / D, accum_out=dst)
 
         banks = {}
         quant = {}
         accs = {}
 
         def stage_t(u):
-            xt = psum.tile([P, 2, 2, P], F32, tag="xt")
-            vt = psum.tile([P, 2, 2, P], F32, tag="vt")
+            vt = psum.tile([P, 2, 2, P], F32, tag="tp", bufs=5)
+            xt = psum.tile([P, 2, 2, P], F32, tag="tp", bufs=5)
             transposes(vt, [xv_of[2 * u], xv_of[2 * u + 1]])
             transposes(xt, [x_of[2 * u], x_of[2 * u + 1]])
             banks[u] = (xt, vt)
@@ -117,9 +111,13 @@ def tile_probprotoseghead_kernel(tc, x, x_var, prototypes, proto_var, out):
             xt, vt = banks[u]
             g = work.tile([P, 2048], BF16, tag="g", align_bytes=64)
             nc.scalar.activation(out=halves_out(g[:, 1024:2048]), in_=as_halves(vt), func=ACT.Sqrt)
-            nc.scalar.copy(
-                out=g[:, 0:1024].bitcast(F32).rearrange("p (m u) -> p m u", u=2), in_=as_words(xt)
-            )
+            if u in V_COPY_UNITS:
+                nc.vector.tensor_copy(out=words_out(g[:, 0:1024]), in_=as_words(xt))
+            else:
+                nc.scalar.copy(out=words_out(g[:, 0:1024]), in_=as_words(xt))
+            for t in (2 * u, 2 * u + 1):
+                if t in S_SUM_TILES:
+                    row_sum_s(bn_s[:, t : t + 1], xv_of[t])
             quant[u] = g
 
         def stage_q(u):
@@ -144,36 +142,56 @@ def tile_probprotoseghead_kernel(tc, x, x_var, prototypes, proto_var, out):
             accs[u] = acc
 
         def stage_sum(u):
-            for i in range(2):
-                t = 2 * u + i
-                row_sum(bn[:, t : t + 1], xv_of[t])
+            for t in (2 * u, 2 * u + 1):
+                if t not in S_SUM_TILES:
+                    row_sum_v(bn_v[:, t : t + 1], xv_of[t])
 
         def stage_e(u):
             acc = accs[u]
             o_sb = work.tile([P, 2, J], F32, tag="o", bufs=4)
             for i in range(2):
                 t = 2 * u + i
+                bn = bn_s if t in S_SUM_TILES else bn_v
                 nc.vector.scalar_tensor_tensor(
                     out=o_sb[:, i, :], in0=acc[:, i, :], scalar=bn[:, t : t + 1], in1=bj[:],
                     op0=ALU.add, op1=ALU.add,
                 )
             nc.sync.dma_start(out=out_v[:, 2 * u : 2 * u + 2, :], in_=o_sb[:])
 
+        pvt = psum.tile([P, 2, 2, P], F32, tag="tp", bufs=5)
+        pt = psum.tile([P, 2, 2, P], F32, tag="tp", bufs=5)
+        transposes(pvt, [pv_sb[:, 0, :], pv_sb[:, 1, :]])
+        transposes(pt, [p_sb[:, 0, :], p_sb[:, 1, :]])
+        nc.scalar.activation(out=halves_out(sq_tmp[:]), in_=as_halves(pvt), func=ACT.Sqrt)
+        for r in range(2):
+            row_sum_v(spn[:, r : r + 1], pv_sb[:, r, :])
+        for r in range(2):
+            nc.vector.tensor_copy(out=rep[:, r, :], in_=spn[:, r : r + 1].to_broadcast([P, P]))
+        nc.vector.tensor_scalar(
+            out=halves_out(gp[:, 0:1024]), in0=as_halves(pt), scalar1=2.0, scalar2=None, op0=ALU.mult
+        )
         stage_t(0)
-        stage_sum(0)
-        bt = psum.tile([P, 2, P], F32, tag="bt", bufs=1)
+        bt = psum.tile([P, 2, P], F32, tag="acc", bufs=3)
         for r in range(2):
             nc.tensor.transpose(bt[:, r, :], rep[:, r, :], ident[:])
         nc.vector.tensor_scalar(
+            out=gp[:, 1024:2048], in0=sq_tmp[:], scalar1=2.0 ** -8, scalar2=None, op0=ALU.mult
+        )
+        nc.vector.quantize_mx(out=p_codes[:].bitcast(FP8X4), scales=p_scl[:], in_=gp[:])
+        nc.vector.tensor_scalar(
             out=bj[:], in0=bt[:].rearrange("p r n -> p (r n)"), scalar1=-2.0, scalar2=None, op0=ALU.add
         )
+        stage_sum(0)
+        stage_t(1)
+        stage_s(0)
+        stage_sum(1)
 
-        for k in range(NU + 2):
+        for k in range(1, NU + 2):
             if k + 1 < NU:
                 stage_t(k + 1)
             if k < NU:
                 stage_s(k)
-            if 1 <= k <= NU:
+            if k <= NU:
                 stage_q(k - 1)
             if k + 1 < NU:
                 stage_sum(k + 1)

@@ -18,7 +18,7 @@ J = 256
 NT = N_PIX // P
 NU = NT // 2
 CHUNKS = (2, 2, 4, 4, 4, 4, 4)
-S_SUM_TILES = (7, 11, 15, 19)
+S_SUM_TILES = ()
 V_COPY_UNITS = ()
 FLOPS = 2 * 2 * N_PIX * J * D
 

@@ -16,10 +16,11 @@ N_PIX = 3072
 D = 512
 J = 256
 NT = N_PIX // P
-NU = NT // 2
 CHUNKS = (2, 2, 4, 4, 4, 4, 4)
-S_SUM_TILES = ()
-V_COPY_UNITS = ()
+GROUPS = (2,) * 12
+S_SUMS_AFTER = {4: (9,), 11: (22, 23)}
+V_COPY_GROUPS = ()
+AHEAD = 1
 FLOPS = 2 * 2 * N_PIX * J * D
 
 
@@ -30,6 +31,9 @@ def tile_probprotoseghead_kernel(tc, x, x_var, prototypes, proto_var, out):
     out_v = out.rearrange("(p t) c m -> p t (c m)", t=NT)
     p_v = prototypes.rearrange("(r c) m d -> (c m) r d", r=2)
     pv_v = proto_var.rearrange("(r c) m d -> (c m) r d", r=2)
+    ng = len(GROUPS)
+    first = [sum(GROUPS[:g]) for g in range(ng)]
+    s_sum_tiles = [t for g in S_SUMS_AFTER for t in S_SUMS_AFTER[g]]
 
     with ExitStack() as ctx:
         keep = ctx.enter_context(tc.tile_pool(name="keep", bufs=1))
@@ -60,15 +64,13 @@ def tile_probprotoseghead_kernel(tc, x, x_var, prototypes, proto_var, out):
         bn_v = keep.tile([P, NT], F32, name="bn_v")
         bn_s = keep.tile([P, NT], F32, name="bn_s")
         spn = keep.tile([P, 2], F32, name="spn")
-        rep = keep.tile([P, 2, P], F32, name="rep")
         bj = keep.tile([P, J], F32, name="bj")
         gp = keep.tile([P, 2048], BF16, name="gp", align_bytes=64)
-        sq_tmp = keep.tile([P, 1024], BF16, name="sq_tmp")
         p_codes = keep.tile([P, 512], U32, name="p_codes", align_bytes=64)
         p_scl = keep.tile([P, 512], U8, name="p_scl", align_bytes=64)
 
         def transposes(bank, rows):
-            for i in range(2):
+            for i in range(len(rows)):
                 words = rows[i].bitcast(F32)
                 for u in range(2):
                     nc.tensor.transpose(bank[:, u, i, :], words[:, u * P : (u + 1) * P], ident[:])
@@ -100,36 +102,41 @@ def tile_probprotoseghead_kernel(tc, x, x_var, prototypes, proto_var, out):
         quant = {}
         accs = {}
 
-        def stage_t(u):
-            vt = psum.tile([P, 2, 2, P], F32, tag="tp", bufs=5)
-            xt = psum.tile([P, 2, 2, P], F32, tag="tp", bufs=5)
-            transposes(vt, [xv_of[2 * u], xv_of[2 * u + 1]])
-            transposes(xt, [x_of[2 * u], x_of[2 * u + 1]])
-            banks[u] = (xt, vt)
+        def tiles_of(g):
+            return list(range(first[g], first[g] + GROUPS[g]))
 
-        def stage_s(u):
-            xt, vt = banks[u]
-            g = work.tile([P, 2048], BF16, tag="g", align_bytes=64)
-            nc.scalar.activation(out=halves_out(g[:, 1024:2048]), in_=as_halves(vt), func=ACT.Sqrt)
-            if u in V_COPY_UNITS:
-                nc.vector.tensor_copy(out=words_out(g[:, 0:1024]), in_=as_words(xt))
+        def stage_t(g):
+            w = GROUPS[g]
+            vt = psum.tile([P, 2, w, P], F32, tag="tp", bufs=5)
+            xt = psum.tile([P, 2, w, P], F32, tag="tp", bufs=5)
+            transposes(vt, [xv_of[t] for t in tiles_of(g)])
+            transposes(xt, [x_of[t] for t in tiles_of(g)])
+            banks[g] = (xt, vt)
+
+        def stage_s(g):
+            w = GROUPS[g]
+            xt, vt = banks[g]
+            grouped = work.tile([P, 2 * w * D], BF16, tag="g%d" % w, align_bytes=64)
+            nc.scalar.activation(out=halves_out(grouped[:, w * D : 2 * w * D]), in_=as_halves(vt), func=ACT.Sqrt)
+            if g in V_COPY_GROUPS:
+                nc.vector.tensor_copy(out=words_out(grouped[:, 0 : w * D]), in_=as_words(xt))
             else:
-                nc.scalar.copy(out=words_out(g[:, 0:1024]), in_=as_words(xt))
-            for t in (2 * u, 2 * u + 1):
-                if t in S_SUM_TILES:
-                    row_sum_s(bn_s[:, t : t + 1], xv_of[t])
-            quant[u] = g
+                nc.scalar.copy(out=words_out(grouped[:, 0 : w * D]), in_=as_words(xt))
+            for t in S_SUMS_AFTER.get(g, ()):
+                row_sum_s(bn_s[:, t : t + 1], xv_of[t])
+            quant[g] = grouped
 
-        def stage_q(u):
-            g = quant[u]
-            codes = work.tile([P, 512], U32, tag="codes", align_bytes=64)
-            scl = work.tile([P, 512], U8, tag="scl", align_bytes=64)
-            nc.vector.quantize_mx(out=codes[:].bitcast(FP8X4), scales=scl[:], in_=g[:])
-            acc = psum.tile([P, 2, J], F32, tag="acc", bufs=3)
-            for i in range(2):
+        def stage_q(g):
+            w = GROUPS[g]
+            grouped = quant[g]
+            codes = work.tile([P, 2 * w * P], U32, tag="codes%d" % w, align_bytes=64)
+            scl = work.tile([P, 2 * w * P], U8, tag="scl%d" % w, align_bytes=64)
+            nc.vector.quantize_mx(out=codes[:].bitcast(FP8X4), scales=scl[:], in_=grouped[:])
+            acc = psum.tile([P, w, J], F32, tag="acc", bufs=3)
+            for i in range(w):
                 for h in range(2):
-                    cols = slice(256 * h + P * i, 256 * h + P * i + P)
-                    pcols = slice(256 * h, 256 * h + 256)
+                    cols = slice(w * P * h + P * i, w * P * h + P * i + P)
+                    pcols = slice(J * h, J * h + J)
                     nc.tensor.matmul_mx(
                         out=acc[:, i, :],
                         lhsT=codes[:, cols].bitcast(FP8X4),
@@ -139,61 +146,61 @@ def tile_probprotoseghead_kernel(tc, x, x_var, prototypes, proto_var, out):
                         start=(h == 0),
                         stop=(h == 1),
                     )
-            accs[u] = acc
+            accs[g] = acc
 
-        def stage_sum(u):
-            for t in (2 * u, 2 * u + 1):
-                if t not in S_SUM_TILES:
+        def stage_sum(g):
+            for t in tiles_of(g):
+                if t not in s_sum_tiles:
                     row_sum_v(bn_v[:, t : t + 1], xv_of[t])
 
-        def stage_e(u):
-            acc = accs[u]
-            o_sb = work.tile([P, 2, J], F32, tag="o", bufs=4)
-            for i in range(2):
-                t = 2 * u + i
-                bn = bn_s if t in S_SUM_TILES else bn_v
+        def stage_e(g):
+            w = GROUPS[g]
+            acc = accs[g]
+            o_sb = work.tile([P, w, J], F32, tag="o%d" % w, bufs=4)
+            for i, t in enumerate(tiles_of(g)):
+                bn = bn_s if t in s_sum_tiles else bn_v
                 nc.vector.scalar_tensor_tensor(
                     out=o_sb[:, i, :], in0=acc[:, i, :], scalar=bn[:, t : t + 1], in1=bj[:],
                     op0=ALU.add, op1=ALU.add,
                 )
-            nc.sync.dma_start(out=out_v[:, 2 * u : 2 * u + 2, :], in_=o_sb[:])
+            nc.sync.dma_start(out=out_v[:, first[g] : first[g] + w, :], in_=o_sb[:])
 
         pvt = psum.tile([P, 2, 2, P], F32, tag="tp", bufs=5)
         pt = psum.tile([P, 2, 2, P], F32, tag="tp", bufs=5)
         transposes(pvt, [pv_sb[:, 0, :], pv_sb[:, 1, :]])
         transposes(pt, [p_sb[:, 0, :], p_sb[:, 1, :]])
-        nc.scalar.activation(out=halves_out(sq_tmp[:]), in_=as_halves(pvt), func=ACT.Sqrt)
         for r in range(2):
             row_sum_v(spn[:, r : r + 1], pv_sb[:, r, :])
-        for r in range(2):
-            nc.vector.tensor_copy(out=rep[:, r, :], in_=spn[:, r : r + 1].to_broadcast([P, P]))
+        nc.scalar.activation(
+            out=halves_out(gp[:, 1024:2048]), in_=as_halves(pvt), func=ACT.Sqrt, scale=2.0 ** -16
+        )
         nc.vector.tensor_scalar(
             out=halves_out(gp[:, 0:1024]), in0=as_halves(pt), scalar1=2.0, scalar2=None, op0=ALU.mult
         )
         stage_t(0)
         bt = psum.tile([P, 2, P], F32, tag="acc", bufs=3)
         for r in range(2):
-            nc.tensor.transpose(bt[:, r, :], rep[:, r, :], ident[:])
-        nc.vector.tensor_scalar(
-            out=gp[:, 1024:2048], in0=sq_tmp[:], scalar1=2.0 ** -8, scalar2=None, op0=ALU.mult
-        )
+            nc.tensor.matmul(
+                out=bt[:, r, :], lhsT=spn[:, r : r + 1].to_broadcast([P, P]), rhs=ident[:], start=True, stop=True
+            )
+        stage_sum(0)
         nc.vector.quantize_mx(out=p_codes[:].bitcast(FP8X4), scales=p_scl[:], in_=gp[:])
+        stage_t(1)
+        stage_s(0)
         nc.vector.tensor_scalar(
             out=bj[:], in0=bt[:].rearrange("p r n -> p (r n)"), scalar1=-2.0, scalar2=None, op0=ALU.add
         )
-        stage_sum(0)
-        stage_t(1)
-        stage_s(0)
-        stage_sum(1)
+        for g in range(1, AHEAD + 1):
+            stage_sum(g)
 
-        for k in range(1, NU + 2):
-            if k + 1 < NU:
+        for k in range(1, ng + 2):
+            if k + 1 < ng:
                 stage_t(k + 1)
-            if k < NU:
+            if k < ng:
                 stage_s(k)
-            if k <= NU:
+            if k <= ng:
                 stage_q(k - 1)
-            if k + 1 < NU:
-                stage_sum(k + 1)
+            if k + AHEAD < ng:
+                stage_sum(k + AHEAD)
             if k >= 2:
                 stage_e(k - 2)

@@ -16,7 +16,7 @@ N_PIX = 3072
 D = 512
 J = 256
 NT = N_PIX // P
-CHUNKS = (2, 2, 4, 4, 4, 4, 4)
+CHUNKS = (2, 2, 4, 4, 4, 4, 2, 2)
 GROUPS = (2,) * 12
 S_SUMS_AFTER = {4: (9,), 11: (22, 23)}
 V_COPY_GROUPS = ()
@@ -163,7 +163,10 @@ def tile_probprotoseghead_kernel(tc, x, x_var, prototypes, proto_var, out):
                     out=o_sb[:, i, :], in0=acc[:, i, :], scalar=bn[:, t : t + 1], in1=bj[:],
                     op0=ALU.add, op1=ALU.add,
                 )
-            nc.sync.dma_start(out=out_v[:, first[g] : first[g] + w, :], in_=o_sb[:])
+                if g == ng - 1:
+                    nc.sync.dma_start(out=out_v[:, t : t + 1, :], in_=o_sb[:, i : i + 1, :])
+            if g < ng - 1:
+                nc.sync.dma_start(out=out_v[:, first[g] : first[g] + w, :], in_=o_sb[:])
 
         pvt = psum.tile([P, 2, 2, P], F32, tag="tp", bufs=5)
         pt = psum.tile([P, 2, 2, P], F32, tag="tp", bufs=5)

@@ -16,7 +16,7 @@ N_PIX = 3072
 D = 512
 J = 256
 NT = N_PIX // P
-CHUNKS = (2, 2, 4, 4, 4, 4, 2, 2)
+CHUNKS = (2, 2, 4, 4, 4, 4, 4)
 GROUPS = (2,) * 12
 S_SUMS_AFTER = {4: (9,), 11: (22, 23)}
 V_COPY_GROUPS = ()
@@ -26,9 +26,9 @@ FLOPS = 2 * 2 * N_PIX * J * D
 
 def tile_probprotoseghead_kernel(tc, x, x_var, prototypes, proto_var, out):
     nc = tc.nc
-    x_v = x.rearrange("(p t) d -> p t d", t=NT)
-    xv_v = x_var.rearrange("(p t) d -> p t d", t=NT)
-    out_v = out.rearrange("(p t) c m -> p t (c m)", t=NT)
+    x_v = x.rearrange("(p t) d -> p (t d)", t=NT)
+    xv_v = x_var.rearrange("(p t) d -> p (t d)", t=NT)
+    out_v = out.rearrange("(p t) c m -> p (t c m)", t=NT)
     p_v = prototypes.rearrange("(r c) m d -> (c m) r d", r=2)
     pv_v = proto_var.rearrange("(r c) m d -> (c m) r d", r=2)
     ng = len(GROUPS)
@@ -49,13 +49,13 @@ def tile_probprotoseghead_kernel(tc, x, x_var, prototypes, proto_var, out):
         xv_of = []
         t0 = 0
         for c, size in enumerate(CHUNKS):
-            xv_c = keep.tile([P, size, D], BF16, name="xv%d" % c)
-            x_c = keep.tile([P, size, D], BF16, name="x%d" % c)
-            nc.sync.dma_start(out=xv_c[:], in_=xv_v[:, t0 : t0 + size, :])
-            nc.sync.dma_start(out=x_c[:], in_=x_v[:, t0 : t0 + size, :])
+            xv_c = keep.tile([P, size * D], BF16, name="xv%d" % c)
+            x_c = keep.tile([P, size * D], BF16, name="x%d" % c)
+            nc.sync.dma_start(out=xv_c[:], in_=xv_v[:, t0 * D : (t0 + size) * D])
+            nc.sync.dma_start(out=x_c[:], in_=x_v[:, t0 * D : (t0 + size) * D])
             for k in range(size):
-                x_of.append(x_c[:, k, :])
-                xv_of.append(xv_c[:, k, :])
+                x_of.append(x_c[:, k * D : (k + 1) * D])
+                xv_of.append(xv_c[:, k * D : (k + 1) * D])
             t0 += size
 
         ident = keep.tile([P, P], F32, name="ident")
@@ -87,10 +87,10 @@ def tile_probprotoseghead_kernel(tc, x, x_var, prototypes, proto_var, out):
         def words_out(ap):
             return ap.bitcast(F32).rearrange("p (m u) -> p m u", u=2)
 
-        def row_sum_v(dst, rows):
+        def row_sum_v(dst, rows, init=None):
             junk = work.tile([P, D], BF16, tag="junk_v")
             nc.vector.tensor_scalar(
-                out=junk[:], in0=rows, scalar1=-1.0 / D, scalar2=None,
+                out=junk[:], in0=rows, scalar1=-1.0 / D, scalar2=init,
                 op0=ALU.mult, op1=ALU.add, accum_out=dst,
             )
 
@@ -156,24 +156,24 @@ def tile_probprotoseghead_kernel(tc, x, x_var, prototypes, proto_var, out):
         def stage_e(g):
             w = GROUPS[g]
             acc = accs[g]
-            o_sb = work.tile([P, w, J], F32, tag="o%d" % w, bufs=4)
+            o_sb = work.tile([P, w * J], F32, tag="o%d" % w, bufs=12)
             for i, t in enumerate(tiles_of(g)):
                 bn = bn_s if t in s_sum_tiles else bn_v
                 nc.vector.scalar_tensor_tensor(
-                    out=o_sb[:, i, :], in0=acc[:, i, :], scalar=bn[:, t : t + 1], in1=bj[:],
+                    out=o_sb[:, i * J : (i + 1) * J], in0=acc[:, i, :], scalar=bn[:, t : t + 1], in1=bj[:],
                     op0=ALU.add, op1=ALU.add,
                 )
                 if g == ng - 1:
-                    nc.sync.dma_start(out=out_v[:, t : t + 1, :], in_=o_sb[:, i : i + 1, :])
+                    nc.sync.dma_start(out=out_v[:, t * J : (t + 1) * J], in_=o_sb[:, i * J : (i + 1) * J])
             if g < ng - 1:
-                nc.sync.dma_start(out=out_v[:, first[g] : first[g] + w, :], in_=o_sb[:])
+                nc.sync.dma_start(out=out_v[:, first[g] * J : (first[g] + w) * J], in_=o_sb[:])
 
         pvt = psum.tile([P, 2, 2, P], F32, tag="tp", bufs=5)
         pt = psum.tile([P, 2, 2, P], F32, tag="tp", bufs=5)
         transposes(pvt, [pv_sb[:, 0, :], pv_sb[:, 1, :]])
         transposes(pt, [p_sb[:, 0, :], p_sb[:, 1, :]])
         for r in range(2):
-            row_sum_v(spn[:, r : r + 1], pv_sb[:, r, :])
+            row_sum_v(spn[:, r : r + 1], pv_sb[:, r, :], init=-2.0)
         nc.scalar.activation(
             out=halves_out(gp[:, 1024:2048]), in_=as_halves(pvt), func=ACT.Sqrt, scale=2.0 ** -16
         )
@@ -190,9 +190,7 @@ def tile_probprotoseghead_kernel(tc, x, x_var, prototypes, proto_var, out):
         nc.vector.quantize_mx(out=p_codes[:].bitcast(FP8X4), scales=p_scl[:], in_=gp[:])
         stage_t(1)
         stage_s(0)
-        nc.vector.tensor_scalar(
-            out=bj[:], in0=bt[:].rearrange("p r n -> p (r n)"), scalar1=-2.0, scalar2=None, op0=ALU.add
-        )
+        nc.scalar.copy(out=bj[:], in_=bt[:].rearrange("p r n -> p (r n)"))
         for g in range(1, AHEAD + 1):
             stage_sum(g)
 

@@ -16,10 +16,12 @@ N_PIX = 3072
 D = 512
 J = 256
 NT = N_PIX // P
-CHUNKS = (2, 2, 4, 4, 4, 4, 4)
+CHUNKS = (2, 2, 2, 2, 4, 6, 6)
 GROUPS = (2,) * 12
-S_SUMS_AFTER = {4: (9,), 11: (22, 23)}
-V_COPY_GROUPS = ()
+S_SUMS_AFTER = {11: (22, 23)}
+T_SUM_GROUPS = (5, 8)
+T_LEAD = 3
+FOLD = 64
 AHEAD = 1
 FLOPS = 2 * 2 * N_PIX * J * D
 
@@ -43,8 +45,6 @@ def tile_probprotoseghead_kernel(tc, x, x_var, prototypes, proto_var, out):
 
         pv_sb = keep.tile([P, 2, D], BF16, name="pv_sb")
         p_sb = keep.tile([P, 2, D], BF16, name="p_sb")
-        nc.sync.dma_start(out=pv_sb[:], in_=pv_v)
-        nc.sync.dma_start(out=p_sb[:], in_=p_v)
         x_of = []
         xv_of = []
         t0 = 0
@@ -52,6 +52,9 @@ def tile_probprotoseghead_kernel(tc, x, x_var, prototypes, proto_var, out):
             xv_c = keep.tile([P, size * D], BF16, name="xv%d" % c)
             x_c = keep.tile([P, size * D], BF16, name="x%d" % c)
             nc.sync.dma_start(out=xv_c[:], in_=xv_v[:, t0 * D : (t0 + size) * D])
+            if c == 0:
+                nc.sync.dma_start(out=pv_sb[:], in_=pv_v)
+                nc.sync.dma_start(out=p_sb[:], in_=p_v)
             nc.sync.dma_start(out=x_c[:], in_=x_v[:, t0 * D : (t0 + size) * D])
             for k in range(size):
                 x_of.append(x_c[:, k * D : (k + 1) * D])
@@ -60,6 +63,8 @@ def tile_probprotoseghead_kernel(tc, x, x_var, prototypes, proto_var, out):
 
         ident = keep.tile([P, P], F32, name="ident")
         make_identity(nc, ident[:])
+        mean_ident = keep.tile([P, P], BF16, name="mean_ident")
+        nc.vector.tensor_scalar(out=mean_ident[:], in0=ident[:], scalar1=-1.0 / D, scalar2=None, op0=ALU.mult)
 
         bn_v = keep.tile([P, NT], F32, name="bn_v")
         bn_s = keep.tile([P, NT], F32, name="bn_s")
@@ -98,33 +103,52 @@ def tile_probprotoseghead_kernel(tc, x, x_var, prototypes, proto_var, out):
             junk = work.tile([P, D], BF16, tag="junk_s")
             nc.scalar.activation(out=junk[:], in_=rows, func=ACT.Copy, scale=-1.0 / D, accum_out=dst)
 
-        banks = {}
+        vbanks = {}
+        xbanks = {}
+        folds = {}
         quant = {}
         accs = {}
 
         def tiles_of(g):
             return list(range(first[g], first[g] + GROUPS[g]))
 
-        def stage_t(g):
-            w = GROUPS[g]
-            vt = psum.tile([P, 2, w, P], F32, tag="tp", bufs=5)
-            xt = psum.tile([P, 2, w, P], F32, tag="tp", bufs=5)
+        def stage_tv(g):
+            vt = psum.tile([P, 2, GROUPS[g], P], F32, tag="tp", bufs=5)
             transposes(vt, [xv_of[t] for t in tiles_of(g)])
-            transposes(xt, [x_of[t] for t in tiles_of(g)])
-            banks[g] = (xt, vt)
+            vbanks[g] = vt
 
-        def stage_s(g):
+        def stage_tx(g):
+            xt = psum.tile([P, 2, GROUPS[g], P], F32, tag="tp", bufs=5)
+            transposes(xt, [x_of[t] for t in tiles_of(g)])
+            xbanks[g] = xt
+
+        def stage_sv(g):
             w = GROUPS[g]
-            xt, vt = banks[g]
             grouped = work.tile([P, 2 * w * D], BF16, tag="g%d" % w, align_bytes=64)
-            nc.scalar.activation(out=halves_out(grouped[:, w * D : 2 * w * D]), in_=as_halves(vt), func=ACT.Sqrt)
-            if g in V_COPY_GROUPS:
-                nc.vector.tensor_copy(out=words_out(grouped[:, 0 : w * D]), in_=as_words(xt))
-            else:
-                nc.scalar.copy(out=words_out(grouped[:, 0 : w * D]), in_=as_words(xt))
+            nc.scalar.activation(out=halves_out(grouped[:, w * D : 2 * w * D]), in_=as_halves(vbanks[g]), func=ACT.Sqrt)
+            quant[g] = grouped
+
+        def stage_sx(g):
+            w = GROUPS[g]
+            nc.scalar.copy(out=words_out(quant[g][:, 0 : w * D]), in_=as_words(xbanks[g]))
             for t in S_SUMS_AFTER.get(g, ()):
                 row_sum_s(bn_s[:, t : t + 1], xv_of[t])
-            quant[g] = grouped
+
+        def stage_fold(k):
+            for g in T_SUM_GROUPS:
+                for i, t in enumerate(tiles_of(g)):
+                    if k != g - T_LEAD + i:
+                        continue
+                    if i == 0:
+                        folds[g] = psum.tile([P, 2, FOLD], F32, tag="fold", name="fold", bufs=1)
+                    for c in range(D // FOLD):
+                        nc.tensor.matmul(
+                            out=folds[g][:, i, :],
+                            lhsT=mean_ident[:],
+                            rhs=xv_of[t][:, c * FOLD : (c + 1) * FOLD],
+                            start=(c == 0),
+                            stop=(c == D // FOLD - 1),
+                        )
 
         def stage_q(g):
             w = GROUPS[g]
@@ -132,7 +156,7 @@ def tile_probprotoseghead_kernel(tc, x, x_var, prototypes, proto_var, out):
             codes = work.tile([P, 2 * w * P], U32, tag="codes%d" % w, align_bytes=64)
             scl = work.tile([P, 2 * w * P], U8, tag="scl%d" % w, align_bytes=64)
             nc.vector.quantize_mx(out=codes[:].bitcast(FP8X4), scales=scl[:], in_=grouped[:])
-            acc = psum.tile([P, w, J], F32, tag="acc", bufs=3)
+            acc = psum.tile([P, w, J], F32, tag="acc", bufs=2)
             for i in range(w):
                 for h in range(2):
                     cols = slice(w * P * h + P * i, w * P * h + P * i + P)
@@ -149,6 +173,11 @@ def tile_probprotoseghead_kernel(tc, x, x_var, prototypes, proto_var, out):
             accs[g] = acc
 
         def stage_sum(g):
+            if g in T_SUM_GROUPS:
+                nc.vector.tensor_reduce(
+                    out=bn_v[:, first[g] : first[g] + 2], in_=folds[g][:], axis=mybir.AxisListType.X, op=ALU.add
+                )
+                return
             for t in tiles_of(g):
                 if t not in s_sum_tiles:
                     row_sum_v(bn_v[:, t : t + 1], xv_of[t])
@@ -168,6 +197,9 @@ def tile_probprotoseghead_kernel(tc, x, x_var, prototypes, proto_var, out):
             if g < ng - 1:
                 nc.sync.dma_start(out=out_v[:, first[g] * J : (first[g] + w) * J], in_=o_sb[:])
 
+        stage_tv(0)
+        stage_sv(0)
+        stage_sum(0)
         pvt = psum.tile([P, 2, 2, P], F32, tag="tp", bufs=5)
         pt = psum.tile([P, 2, 2, P], F32, tag="tp", bufs=5)
         transposes(pvt, [pv_sb[:, 0, :], pv_sb[:, 1, :]])
@@ -180,27 +212,30 @@ def tile_probprotoseghead_kernel(tc, x, x_var, prototypes, proto_var, out):
         nc.vector.tensor_scalar(
             out=halves_out(gp[:, 0:1024]), in0=as_halves(pt), scalar1=2.0, scalar2=None, op0=ALU.mult
         )
-        stage_t(0)
-        bt = psum.tile([P, 2, P], F32, tag="acc", bufs=3)
+        stage_tx(0)
+        bt = psum.tile([P, 2, P], F32, tag="acc", bufs=2)
         for r in range(2):
             nc.tensor.matmul(
                 out=bt[:, r, :], lhsT=spn[:, r : r + 1].to_broadcast([P, P]), rhs=ident[:], start=True, stop=True
             )
-        stage_sum(0)
-        nc.vector.quantize_mx(out=p_codes[:].bitcast(FP8X4), scales=p_scl[:], in_=gp[:])
-        stage_t(1)
-        stage_s(0)
+        stage_tv(1)
+        stage_tx(1)
+        stage_sx(0)
         nc.scalar.copy(out=bj[:], in_=bt[:].rearrange("p r n -> p (r n)"))
+        nc.vector.quantize_mx(out=p_codes[:].bitcast(FP8X4), scales=p_scl[:], in_=gp[:])
         for g in range(1, AHEAD + 1):
             stage_sum(g)
 
         for k in range(1, ng + 2):
             if k + 1 < ng:
-                stage_t(k + 1)
+                stage_tv(k + 1)
+                stage_tx(k + 1)
             if k < ng:
-                stage_s(k)
+                stage_sv(k)
+                stage_sx(k)
             if k <= ng:
                 stage_q(k - 1)
+            stage_fold(k)
             if k + AHEAD < ng:
                 stage_sum(k + AHEAD)
             if k >= 2:

from contextlib import ExitStack

import concourse.mybir as mybir
from concourse.masks import make_identity

F32 = mybir.dt.float32
BF16 = mybir.dt.bfloat16
U32 = mybir.dt.uint32
U8 = mybir.dt.uint8
FP8X4 = mybir.dt.float8_e4m3fn_x4
ALU = mybir.AluOpType
ACT = mybir.ActivationFunctionType

P = 128
N_PIX = 3072
D = 512
J = 256
NT = N_PIX // P
CHUNKS = (2, 2, 2, 2, 4, 6, 6)
GROUPS = (2,) * 12
S_SUMS_AFTER = {11: (22, 23)}
T_SUM_GROUPS = (5, 8)
T_LEAD = 3
FOLD = 64
AHEAD = 1
FLOPS = 2 * 2 * N_PIX * J * D


def tile_probprotoseghead_kernel(tc, x, x_var, prototypes, proto_var, out):
    nc = tc.nc
    x_v = x.rearrange("(p t) d -> p (t d)", t=NT)
    xv_v = x_var.rearrange("(p t) d -> p (t d)", t=NT)
    out_v = out.rearrange("(p t) c m -> p (t c m)", t=NT)
    p_v = prototypes.rearrange("(r c) m d -> (c m) r d", r=2)
    pv_v = proto_var.rearrange("(r c) m d -> (c m) r d", r=2)
    ng = len(GROUPS)
    first = [sum(GROUPS[:g]) for g in range(ng)]
    s_sum_tiles = [t for g in S_SUMS_AFTER for t in S_SUMS_AFTER[g]]

    with ExitStack() as ctx:
        keep = ctx.enter_context(tc.tile_pool(name="keep", bufs=1))
        work = ctx.enter_context(tc.tile_pool(name="work", bufs=3))
        psum = ctx.enter_context(tc.psum_pool(name="psum", bufs=2))
        ctx.enter_context(tc.manual_schedule())

        pv_sb = keep.tile([P, 2, D], BF16, name="pv_sb")
        p_sb = keep.tile([P, 2, D], BF16, name="p_sb")
        x_of = []
        xv_of = []
        t0 = 0
        for c, size in enumerate(CHUNKS):
            xv_c = keep.tile([P, size * D], BF16, name="xv%d" % c)
            x_c = keep.tile([P, size * D], BF16, name="x%d" % c)
            nc.sync.dma_start(out=xv_c[:], in_=xv_v[:, t0 * D : (t0 + size) * D])
            if c == 0:
                nc.sync.dma_start(out=pv_sb[:], in_=pv_v)
                nc.sync.dma_start(out=p_sb[:], in_=p_v)
            nc.sync.dma_start(out=x_c[:], in_=x_v[:, t0 * D : (t0 + size) * D])
            for k in range(size):
                x_of.append(x_c[:, k * D : (k + 1) * D])
                xv_of.append(xv_c[:, k * D : (k + 1) * D])
            t0 += size

        ident = keep.tile([P, P], F32, name="ident")
        make_identity(nc, ident[:])
        mean_ident = keep.tile([P, P], BF16, name="mean_ident")
        nc.vector.tensor_scalar(out=mean_ident[:], in0=ident[:], scalar1=-1.0 / D, scalar2=None, op0=ALU.mult)

        bn_v = keep.tile([P, NT], F32, name="bn_v")
        bn_s = keep.tile([P, NT], F32, name="bn_s")
        spn = keep.tile([P, 2], F32, name="spn")
        bj = keep.tile([P, J], F32, name="bj")
        gp = keep.tile([P, 2048], BF16, name="gp", align_bytes=64)
        p_codes = keep.tile([P, 512], U32, name="p_codes", align_bytes=64)
        p_scl = keep.tile([P, 512], U8, name="p_scl", align_bytes=64)

        def transposes(bank, rows):
            for i in range(len(rows)):
                words = rows[i].bitcast(F32)
                for u in range(2):
                    nc.tensor.transpose(bank[:, u, i, :], words[:, u * P : (u + 1) * P], ident[:])

        def as_words(bank):
            return bank[:].rearrange("p u i n -> p (i n) u")

        def as_halves(bank):
            return bank[:].bitcast(BF16).rearrange("p u i (n e) -> p (i n) u e", e=2)

        def halves_out(ap):
            return ap.rearrange("p (m u e) -> p m u e", u=2, e=2)

        def words_out(ap):
            return ap.bitcast(F32).rearrange("p (m u) -> p m u", u=2)

        def row_sum_v(dst, rows, init=None):
            junk = work.tile([P, D], BF16, tag="junk_v")
            nc.vector.tensor_scalar(
                out=junk[:], in0=rows, scalar1=-1.0 / D, scalar2=init,
                op0=ALU.mult, op1=ALU.add, accum_out=dst,
            )

        def row_sum_s(dst, rows):
            junk = work.tile([P, D], BF16, tag="junk_s")
            nc.scalar.activation(out=junk[:], in_=rows, func=ACT.Copy, scale=-1.0 / D, accum_out=dst)

        vbanks = {}
        xbanks = {}
        folds = {}
        quant = {}
        accs = {}

        def tiles_of(g):
            return list(range(first[g], first[g] + GROUPS[g]))

        def stage_tv(g):
            vt = psum.tile([P, 2, GROUPS[g], P], F32, tag="tp", bufs=5)
            transposes(vt, [xv_of[t] for t in tiles_of(g)])
            vbanks[g] = vt

        def stage_tx(g):
            xt = psum.tile([P, 2, GROUPS[g], P], F32, tag="tp", bufs=5)
            transposes(xt, [x_of[t] for t in tiles_of(g)])
            xbanks[g] = xt

        def stage_sv(g):
            w = GROUPS[g]
            grouped = work.tile([P, 2 * w * D], BF16, tag="g%d" % w, align_bytes=64)
            nc.scalar.activation(out=halves_out(grouped[:, w * D : 2 * w * D]), in_=as_halves(vbanks[g]), func=ACT.Sqrt)
            quant[g] = grouped

        def stage_sx(g):
            w = GROUPS[g]
            nc.scalar.copy(out=words_out(quant[g][:, 0 : w * D]), in_=as_words(xbanks[g]))
            for t in S_SUMS_AFTER.get(g, ()):
                row_sum_s(bn_s[:, t : t + 1], xv_of[t])

        def stage_fold(k):
            for g in T_SUM_GROUPS:
                for i, t in enumerate(tiles_of(g)):
                    if k != g - T_LEAD + i:
                        continue
                    if i == 0:
                        folds[g] = psum.tile([P, 2, FOLD], F32, tag="fold", name="fold", bufs=1)
                    for c in range(D // FOLD):
                        nc.tensor.matmul(
                            out=folds[g][:, i, :],
                            lhsT=mean_ident[:],
                            rhs=xv_of[t][:, c * FOLD : (c + 1) * FOLD],
                            start=(c == 0),
                            stop=(c == D // FOLD - 1),
                        )

        def stage_q(g):
            w = GROUPS[g]
            grouped = quant[g]
            codes = work.tile([P, 2 * w * P], U32, tag="codes%d" % w, align_bytes=64)
            scl = work.tile([P, 2 * w * P], U8, tag="scl%d" % w, align_bytes=64)
            nc.vector.quantize_mx(out=codes[:].bitcast(FP8X4), scales=scl[:], in_=grouped[:])
            acc = psum.tile([P, w, J], F32, tag="acc", bufs=2)
            for i in range(w):
                for h in range(2):
                    cols = slice(w * P * h + P * i, w * P * h + P * i + P)
                    pcols = slice(J * h, J * h + J)
                    nc.tensor.matmul_mx(
                        out=acc[:, i, :],
                        lhsT=codes[:, cols].bitcast(FP8X4),
                        lhsT_scale=scl[:, cols],
                        rhs=p_codes[:, pcols].bitcast(FP8X4),
                        rhs_scale=p_scl[:, pcols],
                        start=(h == 0),
                        stop=(h == 1),
                    )
            accs[g] = acc

        def stage_sum(g):
            if g in T_SUM_GROUPS:
                nc.vector.tensor_reduce(
                    out=bn_v[:, first[g] : first[g] + 2], in_=folds[g][:], axis=mybir.AxisListType.X, op=ALU.add
                )
                return
            for t in tiles_of(g):
                if t not in s_sum_tiles:
                    row_sum_v(bn_v[:, t : t + 1], xv_of[t])

        def stage_e(g):
            w = GROUPS[g]
            acc = accs[g]
            o_sb = work.tile([P, w * J], F32, tag="o%d" % w, bufs=12)
            for i, t in enumerate(tiles_of(g)):
                bn = bn_s if t in s_sum_tiles else bn_v
                nc.vector.scalar_tensor_tensor(
                    out=o_sb[:, i * J : (i + 1) * J], in0=acc[:, i, :], scalar=bn[:, t : t + 1], in1=bj[:],
                    op0=ALU.add, op1=ALU.add,
                )
                if g == ng - 1:
                    nc.sync.dma_start(out=out_v[:, t * J : (t + 1) * J], in_=o_sb[:, i * J : (i + 1) * J])
            if g < ng - 1:
                nc.sync.dma_start(out=out_v[:, first[g] * J : (first[g] + w) * J], in_=o_sb[:])

        stage_tv(0)
        stage_sv(0)
        stage_sum(0)
        pvt = psum.tile([P, 2, 2, P], F32, tag="tp", bufs=5)
        pt = psum.tile([P, 2, 2, P], F32, tag="tp", bufs=5)
        transposes(pvt, [pv_sb[:, 0, :], pv_sb[:, 1, :]])
        transposes(pt, [p_sb[:, 0, :], p_sb[:, 1, :]])
        for r in range(2):
            row_sum_v(spn[:, r : r + 1], pv_sb[:, r, :], init=-2.0)
        nc.scalar.activation(
            out=halves_out(gp[:, 1024:2048]), in_=as_halves(pvt), func=ACT.Sqrt, scale=2.0 ** -16
        )
        nc.vector.tensor_scalar(
            out=halves_out(gp[:, 0:1024]), in0=as_halves(pt), scalar1=2.0, scalar2=None, op0=ALU.mult
        )
        stage_tx(0)
        bt = psum.tile([P, 2, P], F32, tag="acc", bufs=2)
        for r in range(2):
            nc.tensor.matmul(
                out=bt[:, r, :], lhsT=spn[:, r : r + 1].to_broadcast([P, P]), rhs=ident[:], start=True, stop=True
            )
        stage_tv(1)
        stage_tx(1)
        stage_sx(0)
        nc.scalar.copy(out=bj[:], in_=bt[:].rearrange("p r n -> p (r n)"))
        nc.vector.quantize_mx(out=p_codes[:].bitcast(FP8X4), scales=p_scl[:], in_=gp[:])
        for g in range(1, AHEAD + 1):
            stage_sum(g)

        for k in range(1, ng + 2):
            if k + 1 < ng:
                stage_tv(k + 1)
                stage_tx(k + 1)
            if k < ng:
                stage_sv(k)
                stage_sx(k)
            if k <= ng:
                stage_q(k - 1)
            stage_fold(k)
            if k + AHEAD < ng:
                stage_sum(k + AHEAD)
            if k >= 2:
                stage_e(k - 2)
